import numpy as np
import ml_dtypes


def mxq(x, axis, fmt="e4m3"):
    dtype, down = {"e4m3": (ml_dtypes.float8_e4m3fn, 7), "e5m2": (ml_dtypes.float8_e5m2, 14)}[fmt]
    v = np.moveaxis(np.asarray(x, np.float32).astype(ml_dtypes.bfloat16).astype(np.float64), axis, -1)
    blocks = v.reshape(v.shape[:-1] + (-1, 32))
    amax = np.abs(blocks).max(-1, keepdims=True)
    byte = np.maximum(np.where(amax > 0, np.frexp(amax)[1] - 1 + 127, 0) - down, 1)
    scale = np.exp2(byte - 127.0)
    codes = (blocks / scale).astype(np.float32).astype(dtype).astype(np.float64)
    return np.moveaxis((codes * scale).reshape(v.shape), -1, axis)


WIDE = False


def mx_kscale(k):
    if not WIDE:
        return np.ones(k)
    levels = np.array([10, -10, 5, -5, 0])
    a = np.random.permutation(np.resize(levels, k // 512 * 4)).reshape(k // 512, 4)
    idx = np.arange(k)
    return np.exp2(a[idx // 512, idx % 128 // 32])


BF16 = ml_dtypes.bfloat16


def bf(x):
    return np.asarray(x, np.float32).astype(BF16)


def f64(x):
    return np.asarray(x).astype(np.float64)


B, CH, C1, C2, D, NF, W, H = 1, 768, 128, 8192, 1, 8, 8, 8
N = NF * W * H
M = NF * (W // D) * (H // D)


def setup_inputs():
    t = mx_kscale(C2)
    return {"theta": bf(np.tanh(np.random.standard_normal((B, N, C1)) * 0.3)),
            "phi": bf(np.tanh(0.3 + np.random.standard_normal((B, M, C1)) * 0.2)),
            "g": bf((1.0 + np.random.standard_normal((B, M, C2)) * 0.7) * t),
            "x": bf(np.random.standard_normal((B, CH, NF, W, H))),
            "w_attn_g": bf(np.random.standard_normal((CH, C2)) * 2.0 / np.sqrt(C2) / t),
            "b_attn_g": bf(np.random.standard_normal(CH) * 0.2),
            "gamma": bf(0.6 + np.random.standard_normal(1) * 0.2)}


def reference(theta, phi, g, x, w_attn_g, b_attn_g, gamma):
    s = f64(theta) @ f64(phi).transpose(0, 2, 1)
    e = np.exp(s - s.max(axis=1, keepdims=True))
    attn = e / e.sum(axis=1, keepdims=True)
    a = mxq(attn, 2, "e4m3") @ mxq(f64(g), 1, "e4m3")
    y = (mxq(f64(w_attn_g), 1, "e4m3") @ mxq(a.transpose(0, 2, 1), 1, "e4m3")) + f64(b_attn_g)[None, :, None]
    attn_g = y.reshape(B, CH, NF, W, H)
    alpha = 1.0 / (1.0 + np.exp(-f64(gamma)[0]))
    out = (1.0 - alpha) * f64(x) + alpha * attn_g
    return out, attn_g

@@ -1,0 +1,367 @@
+from contextlib import ExitStack
+
+import concourse.mybir as mybir
+from concourse.masks import make_identity
+
+F32 = mybir.dt.float32
+BF16 = mybir.dt.bfloat16
+U32 = mybir.dt.uint32
+U8 = mybir.dt.uint8
+FP8X4 = mybir.dt.float8_e4m3fn_x4
+ACT = mybir.ActivationFunctionType
+ALU = mybir.AluOpType
+
+P = 128
+PACK = 4
+N_Q = 512
+N_K = 512
+C1 = 128
+C2 = 8192
+CH = 768
+CHUNK = P * PACK
+N_CHUNKS = C2 // CHUNK
+UNIT = 2 * CHUNK
+N_UNITS = C2 // UNIT
+N_TILES = CH // P
+EARLY_TILES = 4
+LATE_TILES = N_TILES - EARLY_TILES
+WORK_BANKS = 8 - EARLY_TILES
+EARLY_JOBS = N_UNITS
+LATE_JOBS = LATE_TILES * C2 // (4 * UNIT)
+RAW_BUFS = 3
+
+FLOPS = 2 * N_Q * N_K * C1 + 2 * N_Q * N_K * C2 + 2 * CH * C2 * N_Q
+
+
+def tile_selfattention3d_pa_k_kernel(
+    tc, theta, phi, g, x, w_attn_g, b_attn_g, gamma, out_0, out_1
+):
+    nc = tc.nc
+    with ExitStack() as ctx:
+        ctx.enter_context(tc.manual_schedule())
+        keep = ctx.enter_context(tc.tile_pool(name="keep", bufs=1))
+        raw = ctx.enter_context(tc.tile_pool(name="raw", bufs=RAW_BUFS))
+        grouped = ctx.enter_context(tc.tile_pool(name="grouped", bufs=3))
+        codes = ctx.enter_context(tc.tile_pool(name="codes", bufs=3))
+        results = ctx.enter_context(tc.tile_pool(name="results", bufs=3))
+        y_banks = ctx.enter_context(tc.psum_pool(name="y_banks", bufs=1))
+        work = ctx.enter_context(tc.psum_pool(name="work", bufs=WORK_BANKS))
+
+        theta_rows = theta.rearrange("b (a p) c -> p (b a) c", p=P)
+        phi_rows = phi.rearrange("b (p j) c -> p (b j) c", j=PACK)
+        g_rows = g.rearrange("b (p j) c -> p (b j) c", j=PACK)
+        w_rows = w_attn_g.rearrange("(i p) c -> p i c", p=P)
+        x_rows = x.rearrange("b (i p) f r c -> p (b i) (f r c)", p=P)
+        out_rows = out_0.rearrange("b (i p) f r c -> p (b i) (f r c)", p=P)
+        attn_g_rows = out_1.rearrange("b (i p) f r c -> p (b i) (f r c)", p=P)
+
+        attn_codes = keep.tile([P, N_Q], U32, align_bytes=64)
+        attn_scales = keep.tile([P, N_Q], U8, align_bytes=64)
+        a_codes = keep.tile([P, N_CHUNKS, N_Q], U32, align_bytes=64)
+        a_scales = keep.tile([P, N_CHUNKS, N_Q], U8, align_bytes=64)
+        late_codes = keep.tile([P, 2 * LATE_JOBS, CHUNK], U32, align_bytes=64)
+        late_scales = keep.tile([P, 2 * LATE_JOBS, CHUNK], U8, align_bytes=64)
+        ident_bf16 = keep.tile([P, P], BF16)
+        ident_f32 = keep.tile([P, P], F32)
+        x_sb = keep.tile([P, N_TILES, N_Q], BF16)
+        bias_col = keep.tile([P, N_TILES], F32)
+        alpha = keep.tile([P, 1], F32)
+        one_minus_alpha = keep.tile([P, 1], F32)
+
+        g_raw = {}
+        w_raw = {}
+        g_grouped = {}
+        g_codes = {}
+        a_grouped = {}
+        w_banks = {}
+        w_grouped = {}
+        w_codes = {}
+
+        def load_g(unit):
+            if unit >= N_UNITS:
+                return
+            g_raw[unit] = raw.tile([P, PACK, UNIT], BF16, name="g_raw")
+            nc.sync.dma_start(
+                out=g_raw[unit][:], in_=g_rows[:, :, unit * UNIT : (unit + 1) * UNIT]
+            )
+
+        def load_w(job):
+            if job >= EARLY_JOBS + LATE_JOBS:
+                return
+            w_raw[job] = raw.tile([P, 4 * UNIT], BF16, name="w_raw")
+            if job < EARLY_JOBS:
+                nc.sync.dma_start(
+                    out=w_raw[job][:].rearrange("p (i c) -> p i c", i=EARLY_TILES),
+                    in_=w_rows[:, 0:EARLY_TILES, job * UNIT : (job + 1) * UNIT],
+                )
+            else:
+                first = (job - EARLY_JOBS) * 2 * UNIT
+                nc.sync.dma_start(
+                    out=w_raw[job][:].rearrange("p (i c) -> p i c", i=LATE_TILES),
+                    in_=w_rows[:, EARLY_TILES:N_TILES, first : first + 2 * UNIT],
+                )
+
+        def regroup_g(chunk):
+            if chunk >= N_CHUNKS:
+                return
+            unit, half = divmod(chunk, 2)
+            g_grouped[chunk] = grouped.tile([P, 2, CHUNK // 2, PACK], BF16, name="g_grouped", align_bytes=64)
+            nc.vector.tensor_copy(
+                out=g_grouped[chunk][:],
+                in_=g_raw[unit][:, :, half * CHUNK : (half + 1) * CHUNK].rearrange(
+                    "p j (r e) -> p e r j", e=2
+                ),
+            )
+
+        def quantise_g(chunk):
+            if chunk >= N_CHUNKS:
+                return
+            unit, half = divmod(chunk, 2)
+            if half == 0:
+                words = codes.tile([P, 2, CHUNK], U32, name="g_words", align_bytes=64)
+                scales = codes.tile([P, 2, CHUNK], U8, name="g_scales", align_bytes=64)
+                g_codes[unit] = (words, scales)
+            words, scales = g_codes[unit]
+            nc.vector.quantize_mx(
+                out=words[:, half, :].bitcast(FP8X4),
+                scales=scales[:, half, :],
+                in_=g_grouped[chunk][:].rearrange("p e r j -> p (e r j)"),
+            )
+
+        def transpose_w(job):
+            if job >= EARLY_JOBS + LATE_JOBS:
+                return
+            pairs = w_raw[job][:].bitcast(F32)
+            w_banks[job] = []
+            for k in range(4):
+                bank = work.tile([P, 4, P], F32, name="work")
+                w_banks[job].append(bank)
+                for i in range(2):
+                    if job < EARLY_JOBS:
+                        first = ((k % 2) * 2 + i) * (UNIT // 2) + (k // 2) * (CHUNK // 2)
+                    else:
+                        first = i * UNIT + k * (CHUNK // 2)
+                    for h in range(2):
+                        nc.tensor.transpose(
+                            bank[:, 2 * i + h, :],
+                            pairs[:, first + h * P : first + (h + 1) * P],
+                            ident_f32[:],
+                        )
+
+        def empty_w_banks(job):
+            if job >= EARLY_JOBS + LATE_JOBS:
+                return
+            for k in range(4):
+                if k % 2 == 0:
+                    w_grouped[(job, k // 2)] = grouped.tile([P, 4 * CHUNK], BF16, name="w_grouped", align_bytes=64)
+                target = w_grouped[(job, k // 2)][:].bitcast(F32).rearrange(
+                    "p (k i c h) -> p k i c h", k=2, i=2, h=2
+                )[:, k % 2]
+                source = w_banks[job][k][:].rearrange("p (i h) c -> p i c h", h=2)
+                if job >= EARLY_JOBS and k % 2 == 1:
+                    nc.vector.tensor_copy(out=target, in_=source)
+                else:
+                    nc.scalar.copy(out=target, in_=source)
+
+        def quantise_w(job, half):
+            if job >= EARLY_JOBS + LATE_JOBS:
+                return
+            if job < EARLY_JOBS:
+                if half == 0:
+                    words = codes.tile([P, 2, CHUNK], U32, name="w_words", align_bytes=64)
+                    scales = codes.tile([P, 2, CHUNK], U8, name="w_scales", align_bytes=64)
+                    w_codes[job] = (words, scales)
+                words, scales = w_codes[job]
+                slot = half
+            else:
+                words, scales = late_codes, late_scales
+                slot = 2 * (job - EARLY_JOBS) + half
+            nc.vector.quantize_mx(
+                out=words[:, slot, :].bitcast(FP8X4),
+                scales=scales[:, slot, :],
+                in_=w_grouped[(job, half)][:],
+            )
+
+        def make_a(chunk, block):
+            unit, half = divmod(chunk, 2)
+            words, scales = g_codes[unit]
+            queries = slice(block * P, (block + 1) * P)
+            if block == 0:
+                a_grouped[chunk] = grouped.tile([P, N_Q, PACK], BF16, name="a_grouped", align_bytes=64)
+            bank = work.tile([P, PACK, P], F32, name="work")
+            for t in range(PACK):
+                h, e = divmod(t, 2)
+                columns = slice(e * (CHUNK // 2) + h * P, e * (CHUNK // 2) + (h + 1) * P)
+                nc.tensor.matmul_mx(
+                    out=bank[:, t, :],
+                    lhsT=words[:, half, columns].bitcast(FP8X4),
+                    lhsT_scale=scales[:, half, columns],
+                    rhs=attn_codes[:, queries].bitcast(FP8X4),
+                    rhs_scale=attn_scales[:, queries],
+                    start=True,
+                    stop=True,
+                )
+            nc.scalar.copy(out=a_grouped[chunk][:, queries, :], in_=bank[:].rearrange("p t n -> p n t"))
+
+        def quantise_a(chunk):
+            if chunk < 0 or chunk >= N_CHUNKS:
+                return
+            nc.vector.quantize_mx(
+                out=a_codes[:, chunk, :].bitcast(FP8X4),
+                scales=a_scales[:, chunk, :],
+                in_=a_grouped[chunk][:].rearrange("p n t -> p (n t)"),
+            )
+
+        def project(y, words, scales, chunk):
+            nc.tensor.matmul_mx(
+                out=y[:],
+                lhsT=words.bitcast(FP8X4),
+                lhsT_scale=scales,
+                rhs=a_codes[:, chunk, :].bitcast(FP8X4),
+                rhs_scale=a_scales[:, chunk, :],
+                start=(chunk == 0),
+                stop=(chunk == N_CHUNKS - 1),
+            )
+
+        def project_early(y, i, chunk):
+            words, scales = w_codes[chunk // 2]
+            columns = slice(i * P, (i + 1) * P)
+            project(y, words[:, chunk % 2, columns], scales[:, chunk % 2, columns], chunk)
+
+        def project_late(y, i, chunk):
+            first = (chunk % 2) * LATE_TILES * P + (i - EARLY_TILES) * P
+            columns = slice(first, first + P)
+            project(y, late_codes[:, chunk // 2, columns], late_scales[:, chunk // 2, columns], chunk)
+
+        def finish(y, i):
+            attn_g_sb = results.tile([P, N_Q], F32, name="attn_g_sb")
+            nc.scalar.activation(out=attn_g_sb[:], in_=y[:], func=ACT.Identity, bias=bias_col[:, i : i + 1])
+            nc.sync.dma_start(out=attn_g_rows[:, i, :], in_=attn_g_sb[:])
+            x_part = results.tile([P, N_Q], F32, name="x_part")
+            nc.vector.tensor_scalar(
+                out=x_part[:], in0=x_sb[:, i, :], scalar1=one_minus_alpha[:, 0:1], scalar2=None, op0=ALU.mult
+            )
+            out_sb = results.tile([P, N_Q], F32, name="out_sb")
+            nc.vector.scalar_tensor_tensor(
+                out=out_sb[:], in0=attn_g_sb[:], scalar=alpha[:, 0:1], in1=x_part[:], op0=ALU.mult, op1=ALU.add
+            )
+            nc.sync.dma_start(out=out_rows[:, i, :], in_=out_sb[:])
+
+        theta_sb = keep.tile([P, N_Q // P, C1], BF16)
+        phi_sb = keep.tile([P, PACK, C1], BF16)
+        nc.sync.dma_start(out=phi_sb[:], in_=phi_rows)
+        nc.sync.dma_start(out=theta_sb[:], in_=theta_rows)
+        bias_rows = keep.tile([P, P], BF16)
+        nc.vector.memset(bias_rows[:], 0.0)
+        gamma_sb = keep.tile([P, 1], BF16)
+        for unit in range(RAW_BUFS):
+            load_g(unit)
+            load_w(unit)
+        nc.sync.dma_start(out=bias_rows[0:N_TILES, :], in_=b_attn_g.rearrange("(i c) -> i c", c=P))
+        nc.sync.dma_start(out=gamma_sb[:], in_=gamma.partition_broadcast(P))
+        nc.sync.dma_start(out=x_sb[:], in_=x_rows)
+
+        make_identity(nc, ident_bf16[:])
+        make_identity(nc, ident_f32[:])
+
+        flipped_bank = work.tile([P, 2 * PACK, P], BF16, name="work")
+        for j in range(PACK):
+            nc.tensor.transpose(flipped_bank[:, j, :], phi_sb[:, j, :], ident_bf16[:])
+        for a in range(N_Q // P):
+            nc.tensor.transpose(flipped_bank[:, PACK + a, :], theta_sb[:, a, :], ident_bf16[:])
+        flipped = keep.tile([P, 2 * PACK, P], BF16)
+        nc.vector.tensor_copy(out=flipped[:], in_=flipped_bank[:])
+        theta_t = flipped[:, PACK : 2 * PACK, :].rearrange("c a p -> c (a p)")
+
+        peak = keep.tile([P, PACK], F32)
+        minus_peak = keep.tile([P, PACK], F32)
+        total = keep.tile([P, PACK], F32)
+        one_over_total = keep.tile([P, PACK], F32)
+        exps = keep.tile([P, PACK, N_Q], F32)
+        for j in range(PACK):
+            s_bank = work.tile([P, N_Q], F32, name="work")
+            nc.tensor.matmul(out=s_bank[:], lhsT=flipped[:, j, :], rhs=theta_t, start=True, stop=True)
+            nc.vector.tensor_reduce(out=peak[:, j : j + 1], in_=s_bank[:], axis=mybir.AxisListType.X, op=ALU.max)
+            nc.vector.tensor_scalar_mul(minus_peak[:, j : j + 1], peak[:, j : j + 1], -1.0)
+            nc.scalar.activation(
+                out=exps[:, j, :],
+                in_=s_bank[:],
+                func=ACT.Exp,
+                bias=minus_peak[:, j : j + 1],
+                accum_out=total[:, j : j + 1],
+            )
+        regroup_g(0)
+        nc.vector.reciprocal(one_over_total[:], total[:])
+        attn_grouped = keep.tile([P, N_Q, PACK], BF16, align_bytes=64)
+        nc.vector.tensor_tensor(
+            out=attn_grouped[:],
+            in0=exps[:].rearrange("p j n -> p n j"),
+            in1=one_over_total[:].unsqueeze(1).to_broadcast([P, N_Q, PACK]),
+            op=ALU.mult,
+        )
+        regroup_g(1)
+        load_g(RAW_BUFS)
+        nc.vector.quantize_mx(
+            out=attn_codes[:].bitcast(FP8X4),
+            scales=attn_scales[:],
+            in_=attn_grouped[:].rearrange("p n j -> p (n j)"),
+        )
+        quantise_g(0)
+        quantise_g(1)
+
+        transpose_w(0)
+        load_w(RAW_BUFS)
+        empty_w_banks(0)
+        quantise_w(0, 0)
+        quantise_w(0, 1)
+
+        y_early = []
+        for i in range(EARLY_TILES):
+            y_early.append(y_banks.tile([P, N_Q], F32, name="y%d" % i))
+
+        for k in range(N_UNITS):
+            transpose_w(k + 1)
+            load_w(k + 1 + RAW_BUFS)
+            empty_w_banks(k + 1)
+            regroup_g(2 * k + 2)
+            quantise_a(2 * k - 1)
+            regroup_g(2 * k + 3)
+            load_g(k + 1 + RAW_BUFS)
+            quantise_g(2 * k + 2)
+            quantise_w(k + 1, 0)
+            quantise_g(2 * k + 3)
+            quantise_w(k + 1, 1)
+            for b in range(2 * PACK):
+                make_a(2 * k + b // PACK, b % PACK)
+                if k > 0:
+                    project_early(y_early[b % EARLY_TILES], b % EARLY_TILES, 2 * k - 2 + b // EARLY_TILES)
+            quantise_a(2 * k)
+
+        quantise_a(N_CHUNKS - 1)
+
+        bias_bank = work.tile([P, P], BF16, name="work")
+        nc.tensor.transpose(bias_bank[:], bias_rows[:], ident_bf16[:])
+        nc.vector.tensor_copy(out=bias_col[:], in_=bias_bank[:, 0:N_TILES])
+        exp_minus_gamma = keep.tile([P, 1], F32)
+        nc.scalar.activation(out=exp_minus_gamma[:], in_=gamma_sb[:], func=ACT.Exp, scale=-1.0)
+        nc.vector.tensor_scalar_add(exp_minus_gamma[:], exp_minus_gamma[:], 1.0)
+        nc.vector.reciprocal(alpha[:], exp_minus_gamma[:])
+        nc.vector.tensor_scalar(
+            out=one_minus_alpha[:], in0=alpha[:], scalar1=-1.0, scalar2=1.0, op0=ALU.mult, op1=ALU.add
+        )
+
+        for job in range(EARLY_JOBS + 1, EARLY_JOBS + LATE_JOBS):
+            transpose_w(job)
+            empty_w_banks(job)
+            quantise_w(job, 0)
+            quantise_w(job, 1)
+        for chunk in range(N_CHUNKS - 2, N_CHUNKS):
+            for i in range(EARLY_TILES):
+                project_early(y_early[i], i, chunk)
+        for i in range(EARLY_TILES):
+            finish(y_early[i], i)
+        for i in range(EARLY_TILES, N_TILES):
+            y_late = work.tile([P, N_Q], F32, name="work")
+            for chunk in range(N_CHUNKS):
+                project_late(y_late, i, chunk)
+            finish(y_late, i)

@@ -28,6 +28,7 @@ LATE_TILES = N_TILES - EARLY_TILES
 WORK_BANKS = 8 - EARLY_TILES
 EARLY_JOBS = N_UNITS
 LATE_JOBS = LATE_TILES * C2 // (4 * UNIT)
+LATE_JOBS_FIRST = 2
 RAW_BUFS = 3
 
 FLOPS = 2 * N_Q * N_K * C1 + 2 * N_Q * N_K * C2 + 2 * CH * C2 * N_Q
@@ -107,9 +108,9 @@ def tile_selfattention3d_pa_k_kernel(
             unit, half = divmod(chunk, 2)
             g_grouped[chunk] = grouped.tile([P, 2, CHUNK // 2, PACK], BF16, name="g_grouped", align_bytes=64)
             nc.vector.tensor_copy(
-                out=g_grouped[chunk][:],
+                out=g_grouped[chunk][:].rearrange("p e (c i) j -> p e c j i", i=4),
                 in_=g_raw[unit][:, :, half * CHUNK : (half + 1) * CHUNK].rearrange(
-                    "p j (r e) -> p e r j", e=2
+                    "p j (c i e) -> p e c j i", i=4, e=2
                 ),
             )
 
@@ -153,12 +154,14 @@ def tile_selfattention3d_pa_k_kernel(
                 return
             for k in range(4):
                 if k % 2 == 0:
-                    w_grouped[(job, k // 2)] = grouped.tile([P, 4 * CHUNK], BF16, name="w_grouped", align_bytes=64)
+                    w_grouped[(job, k // 2)] = grouped.tile(
+                        [P, 4 * CHUNK], BF16, name="w_grouped", align_bytes=64, bufs=2 * LATE_JOBS_FIRST + 1
+                    )
                 target = w_grouped[(job, k // 2)][:].bitcast(F32).rearrange(
                     "p (k i c h) -> p k i c h", k=2, i=2, h=2
                 )[:, k % 2]
                 source = w_banks[job][k][:].rearrange("p (i h) c -> p i c h", h=2)
-                if job >= EARLY_JOBS and k % 2 == 1:
+                if job >= EARLY_JOBS + LATE_JOBS_FIRST and k % 2 == 1:
                     nc.vector.tensor_copy(out=target, in_=source)
                 else:
                     nc.scalar.copy(out=target, in_=source)
@@ -247,19 +250,24 @@ def tile_selfattention3d_pa_k_kernel(
             )
             nc.sync.dma_start(out=out_rows[:, i, :], in_=out_sb[:])
 
+        job_order = (
+            list(range(EARLY_JOBS, EARLY_JOBS + LATE_JOBS_FIRST))
+            + list(range(EARLY_JOBS))
+            + list(range(EARLY_JOBS + LATE_JOBS_FIRST, EARLY_JOBS + LATE_JOBS))
+        )
+
+        def load_w_at(place):
+            if place < len(job_order):
+                load_w(job_order[place])
+
         theta_sb = keep.tile([P, N_Q // P, C1], BF16)
         phi_sb = keep.tile([P, PACK, C1], BF16)
         nc.sync.dma_start(out=phi_sb[:], in_=phi_rows)
         nc.sync.dma_start(out=theta_sb[:], in_=theta_rows)
-        bias_rows = keep.tile([P, P], BF16)
-        nc.vector.memset(bias_rows[:], 0.0)
-        gamma_sb = keep.tile([P, 1], BF16)
-        for unit in range(RAW_BUFS):
-            load_g(unit)
-            load_w(unit)
-        nc.sync.dma_start(out=bias_rows[0:N_TILES, :], in_=b_attn_g.rearrange("(i c) -> i c", c=P))
-        nc.sync.dma_start(out=gamma_sb[:], in_=gamma.partition_broadcast(P))
-        nc.sync.dma_start(out=x_sb[:], in_=x_rows)
+        load_g(0)
+        for place in range(RAW_BUFS):
+            load_w_at(place)
+        load_g(1)
 
         make_identity(nc, ident_bf16[:])
         make_identity(nc, ident_f32[:])
@@ -270,7 +278,7 @@ def tile_selfattention3d_pa_k_kernel(
         for a in range(N_Q // P):
             nc.tensor.transpose(flipped_bank[:, PACK + a, :], theta_sb[:, a, :], ident_bf16[:])
         flipped = keep.tile([P, 2 * PACK, P], BF16)
-        nc.vector.tensor_copy(out=flipped[:], in_=flipped_bank[:])
+        nc.scalar.copy(out=flipped[:], in_=flipped_bank[:])
         theta_t = flipped[:, PACK : 2 * PACK, :].rearrange("c a p -> c (a p)")
 
         peak = keep.tile([P, PACK], F32)
@@ -279,7 +287,7 @@ def tile_selfattention3d_pa_k_kernel(
         one_over_total = keep.tile([P, PACK], F32)
         exps = keep.tile([P, PACK, N_Q], F32)
         for j in range(PACK):
-            s_bank = work.tile([P, N_Q], F32, name="work")
+            s_bank = y_banks.tile([P, N_Q], F32, name="y%d" % j)
             nc.tensor.matmul(out=s_bank[:], lhsT=flipped[:, j, :], rhs=theta_t, start=True, stop=True)
             nc.vector.tensor_reduce(out=peak[:, j : j + 1], in_=s_bank[:], axis=mybir.AxisListType.X, op=ALU.max)
             nc.vector.tensor_scalar_mul(minus_peak[:, j : j + 1], peak[:, j : j + 1], -1.0)
@@ -290,54 +298,84 @@ def tile_selfattention3d_pa_k_kernel(
                 bias=minus_peak[:, j : j + 1],
                 accum_out=total[:, j : j + 1],
             )
+        for place in range(LATE_JOBS_FIRST):
+            transpose_w(job_order[place])
+            load_w_at(place + RAW_BUFS)
+            empty_w_banks(job_order[place])
+            if place == 0:
+                load_g(2)
+
+        attn_grouped = keep.tile([P, N_Q, PACK], BF16, align_bytes=64)
+
+        def normalise(block):
+            queries = slice(block * P, (block + 1) * P)
+            nc.vector.tensor_tensor(
+                out=attn_grouped[:, queries, :],
+                in0=exps[:, :, queries].rearrange("p j n -> p n j"),
+                in1=one_over_total[:].unsqueeze(1).to_broadcast([P, P, PACK]),
+                op=ALU.mult,
+            )
+
+        def quantise_attn(block):
+            queries = slice(block * P, (block + 1) * P)
+            nc.vector.quantize_mx(
+                out=attn_codes[:, queries].bitcast(FP8X4),
+                scales=attn_scales[:, queries],
+                in_=attn_grouped[:, queries, :].rearrange("p n j -> p (n j)"),
+            )
+
         regroup_g(0)
         nc.vector.reciprocal(one_over_total[:], total[:])
-        attn_grouped = keep.tile([P, N_Q, PACK], BF16, align_bytes=64)
-        nc.vector.tensor_tensor(
-            out=attn_grouped[:],
-            in0=exps[:].rearrange("p j n -> p n j"),
-            in1=one_over_total[:].unsqueeze(1).to_broadcast([P, N_Q, PACK]),
-            op=ALU.mult,
-        )
+        normalise(0)
+        quantise_g(0)
+        normalise(1)
+        quantise_attn(0)
+        normalise(2)
+        quantise_attn(1)
+        normalise(3)
+        quantise_attn(2)
         regroup_g(1)
         load_g(RAW_BUFS)
-        nc.vector.quantize_mx(
-            out=attn_codes[:].bitcast(FP8X4),
-            scales=attn_scales[:],
-            in_=attn_grouped[:].rearrange("p n j -> p (n j)"),
-        )
-        quantise_g(0)
+        quantise_attn(3)
         quantise_g(1)
-
-        transpose_w(0)
-        load_w(RAW_BUFS)
-        empty_w_banks(0)
-        quantise_w(0, 0)
-        quantise_w(0, 1)
+        for place in range(LATE_JOBS_FIRST):
+            quantise_w(job_order[place], 0)
+            quantise_w(job_order[place], 1)
 
         y_early = []
         for i in range(EARLY_TILES):
             y_early.append(y_banks.tile([P, N_Q], F32, name="y%d" % i))
 
         for k in range(N_UNITS):
-            transpose_w(k + 1)
-            load_w(k + 1 + RAW_BUFS)
-            empty_w_banks(k + 1)
             regroup_g(2 * k + 2)
             quantise_a(2 * k - 1)
             regroup_g(2 * k + 3)
             load_g(k + 1 + RAW_BUFS)
             quantise_g(2 * k + 2)
-            quantise_w(k + 1, 0)
-            quantise_g(2 * k + 3)
-            quantise_w(k + 1, 1)
-            for b in range(2 * PACK):
-                make_a(2 * k + b // PACK, b % PACK)
-                if k > 0:
-                    project_early(y_early[b % EARLY_TILES], b % EARLY_TILES, 2 * k - 2 + b // EARLY_TILES)
-            quantise_a(2 * k)
+            for half in range(2):
+                for b in range(PACK):
+                    make_a(2 * k + half, b)
+                    if k > 0:
+                        project_early(y_early[b], b, 2 * k - 2 + half)
+                if half == 0:
+                    quantise_a(2 * k)
+                    transpose_w(k)
+                    load_w_at(LATE_JOBS_FIRST + k + RAW_BUFS)
+                    empty_w_banks(k)
+                    quantise_g(2 * k + 3)
+                    quantise_w(k, 0)
+                    quantise_w(k, 1)
+            if k == 0:
+                bias_rows = keep.tile([P, P], BF16)
+                nc.vector.memset(bias_rows[:], 0.0)
+                gamma_sb = keep.tile([P, 1], BF16)
+                nc.sync.dma_start(out=bias_rows[0:N_TILES, :], in_=b_attn_g.rearrange("(i c) -> i c", c=P))
+                nc.sync.dma_start(out=gamma_sb[:], in_=gamma.partition_broadcast(P))
+                nc.sync.dma_start(out=x_sb[:], in_=x_rows)
 
         quantise_a(N_CHUNKS - 1)
+        for i in range(EARLY_TILES):
+            project_early(y_early[i], i, N_CHUNKS - 2)
 
         bias_bank = work.tile([P, P], BF16, name="work")
         nc.tensor.transpose(bias_bank[:], bias_rows[:], ident_bf16[:])
@@ -350,14 +388,13 @@ def tile_selfattention3d_pa_k_kernel(
             out=one_minus_alpha[:], in0=alpha[:], scalar1=-1.0, scalar2=1.0, op0=ALU.mult, op1=ALU.add
         )
 
-        for job in range(EARLY_JOBS + 1, EARLY_JOBS + LATE_JOBS):
+        for job in range(EARLY_JOBS + LATE_JOBS_FIRST, EARLY_JOBS + LATE_JOBS):
             transpose_w(job)
             empty_w_banks(job)
             quantise_w(job, 0)
             quantise_w(job, 1)
-        for chunk in range(N_CHUNKS - 2, N_CHUNKS):
-            for i in range(EARLY_TILES):
-                project_early(y_early[i], i, chunk)
+        for i in range(EARLY_TILES):
+            project_early(y_early[i], i, N_CHUNKS - 1)
         for i in range(EARLY_TILES):
             finish(y_early[i], i)
         for i in range(EARLY_TILES, N_TILES):

@@ -78,13 +78,17 @@ def tile_selfattention3d_pa_k_kernel(
         w_grouped = {}
         w_codes = {}
 
-        def load_g(unit):
+        def load_g(unit, pieces=1):
             if unit >= N_UNITS:
                 return
             g_raw[unit] = raw.tile([P, PACK, UNIT], BF16, name="g_raw")
-            nc.sync.dma_start(
-                out=g_raw[unit][:], in_=g_rows[:, :, unit * UNIT : (unit + 1) * UNIT]
-            )
+            width = UNIT // pieces
+            for piece in range(pieces):
+                columns = slice(piece * width, (piece + 1) * width)
+                nc.sync.dma_start(
+                    out=g_raw[unit][:, :, columns],
+                    in_=g_rows[:, :, unit * UNIT + piece * width : unit * UNIT + (piece + 1) * width],
+                )
 
         def load_w(job):
             if job >= EARLY_JOBS + LATE_JOBS:
@@ -264,7 +268,7 @@ def tile_selfattention3d_pa_k_kernel(
         phi_sb = keep.tile([P, PACK, C1], BF16)
         nc.sync.dma_start(out=phi_sb[:], in_=phi_rows)
         nc.sync.dma_start(out=theta_sb[:], in_=theta_rows)
-        load_g(0)
+        load_g(0, pieces=2)
         for place in range(RAW_BUFS):
             load_w_at(place)
         load_g(1)
@@ -272,30 +276,37 @@ def tile_selfattention3d_pa_k_kernel(
         make_identity(nc, ident_bf16[:])
         make_identity(nc, ident_f32[:])
 
-        flipped_bank = work.tile([P, 2 * PACK, P], BF16, name="work")
+        phi_bank = work.tile([P, PACK, P], BF16, name="work")
         for j in range(PACK):
-            nc.tensor.transpose(flipped_bank[:, j, :], phi_sb[:, j, :], ident_bf16[:])
+            nc.tensor.transpose(phi_bank[:, j, :], phi_sb[:, j, :], ident_bf16[:])
+        theta_bank = work.tile([P, N_Q // P, P], BF16, name="work")
         for a in range(N_Q // P):
-            nc.tensor.transpose(flipped_bank[:, PACK + a, :], theta_sb[:, a, :], ident_bf16[:])
-        flipped = keep.tile([P, 2 * PACK, P], BF16)
-        nc.scalar.copy(out=flipped[:], in_=flipped_bank[:])
-        theta_t = flipped[:, PACK : 2 * PACK, :].rearrange("c a p -> c (a p)")
+            nc.tensor.transpose(theta_bank[:, a, :], theta_sb[:, a, :], ident_bf16[:])
+        minus_phi_t = keep.tile([P, PACK, P], BF16)
+        nc.vector.tensor_scalar(
+            out=minus_phi_t[:], in0=phi_bank[:], scalar1=-1.0, scalar2=None, op0=ALU.mult
+        )
+        theta_t = keep.tile([P, N_Q], BF16)
+        nc.scalar.copy(out=theta_t[:], in_=theta_bank[:].rearrange("c a p -> c (a p)"))
 
-        peak = keep.tile([P, PACK], F32)
+        regroup_g(0)
+
         minus_peak = keep.tile([P, PACK], F32)
         total = keep.tile([P, PACK], F32)
         one_over_total = keep.tile([P, PACK], F32)
         exps = keep.tile([P, PACK, N_Q], F32)
         for j in range(PACK):
             s_bank = y_banks.tile([P, N_Q], F32, name="y%d" % j)
-            nc.tensor.matmul(out=s_bank[:], lhsT=flipped[:, j, :], rhs=theta_t, start=True, stop=True)
-            nc.vector.tensor_reduce(out=peak[:, j : j + 1], in_=s_bank[:], axis=mybir.AxisListType.X, op=ALU.max)
-            nc.vector.tensor_scalar_mul(minus_peak[:, j : j + 1], peak[:, j : j + 1], -1.0)
+            nc.tensor.matmul(out=s_bank[:], lhsT=minus_phi_t[:, j, :], rhs=theta_t[:], start=True, stop=True)
+            nc.vector.tensor_reduce(
+                out=minus_peak[:, j : j + 1], in_=s_bank[:], axis=mybir.AxisListType.X, op=ALU.min
+            )
             nc.scalar.activation(
                 out=exps[:, j, :],
                 in_=s_bank[:],
                 func=ACT.Exp,
                 bias=minus_peak[:, j : j + 1],
+                scale=-1.0,
                 accum_out=total[:, j : j + 1],
             )
         for place in range(LATE_JOBS_FIRST):
@@ -324,10 +335,9 @@ def tile_selfattention3d_pa_k_kernel(
                 in_=attn_grouped[:, queries, :].rearrange("p n j -> p (n j)"),
             )
 
-        regroup_g(0)
+        quantise_g(0)
         nc.vector.reciprocal(one_over_total[:], total[:])
         normalise(0)
-        quantise_g(0)
         normalise(1)
         quantise_attn(0)
         normalise(2)

@@ -165,7 +165,7 @@ def tile_selfattention3d_pa_k_kernel(
                     "p (k i c h) -> p k i c h", k=2, i=2, h=2
                 )[:, k % 2]
                 source = w_banks[job][k][:].rearrange("p (i h) c -> p i c h", h=2)
-                if job >= EARLY_JOBS + LATE_JOBS_FIRST and k % 2 == 1:
+                if job >= EARLY_JOBS + LATE_JOBS_FIRST and k % 2 == 1 or job < EARLY_JOBS and k == 3:
                     nc.vector.tensor_copy(out=target, in_=source)
                 else:
                     nc.scalar.copy(out=target, in_=source)

@@ -28,7 +28,6 @@ LATE_TILES = N_TILES - EARLY_TILES
 WORK_BANKS = 8 - EARLY_TILES
 EARLY_JOBS = N_UNITS
 LATE_JOBS = LATE_TILES * C2 // (4 * UNIT)
-LATE_JOBS_FIRST = 2
 RAW_BUFS = 3
 
 FLOPS = 2 * N_Q * N_K * C1 + 2 * N_Q * N_K * C2 + 2 * CH * C2 * N_Q
@@ -78,17 +77,16 @@ def tile_selfattention3d_pa_k_kernel(
         w_grouped = {}
         w_codes = {}
 
-        def load_g(unit, pieces=1):
+        def load_g(unit, piece=0, pieces=1):
             if unit >= N_UNITS:
                 return
-            g_raw[unit] = raw.tile([P, PACK, UNIT], BF16, name="g_raw")
+            if piece == 0:
+                g_raw[unit] = raw.tile([P, PACK, UNIT], BF16, name="g_raw")
             width = UNIT // pieces
-            for piece in range(pieces):
-                columns = slice(piece * width, (piece + 1) * width)
-                nc.sync.dma_start(
-                    out=g_raw[unit][:, :, columns],
-                    in_=g_rows[:, :, unit * UNIT + piece * width : unit * UNIT + (piece + 1) * width],
-                )
+            nc.sync.dma_start(
+                out=g_raw[unit][:, :, piece * width : (piece + 1) * width],
+                in_=g_rows[:, :, unit * UNIT + piece * width : unit * UNIT + (piece + 1) * width],
+            )
 
         def load_w(job):
             if job >= EARLY_JOBS + LATE_JOBS:
@@ -106,11 +104,21 @@ def tile_selfattention3d_pa_k_kernel(
                     in_=w_rows[:, EARLY_TILES:N_TILES, first : first + 2 * UNIT],
                 )
 
-        def regroup_g(chunk):
+        def regroup_g(chunk, on_gpsimd=False):
             if chunk >= N_CHUNKS:
                 return
             unit, half = divmod(chunk, 2)
             g_grouped[chunk] = grouped.tile([P, 2, CHUNK // 2, PACK], BF16, name="g_grouped", align_bytes=64)
+            if on_gpsimd:
+                nc.gpsimd.tensor_scalar(
+                    out=g_grouped[chunk][:],
+                    in0=g_raw[unit][:, :, half * CHUNK : (half + 1) * CHUNK].rearrange("p j (c e) -> p e c j", e=2),
+                    scalar1=1.0,
+                    scalar2=0.0,
+                    op0=ALU.mult,
+                    op1=ALU.add,
+                )
+                return
             nc.vector.tensor_copy(
                 out=g_grouped[chunk][:].rearrange("p e (c i) j -> p e c j i", i=4),
                 in_=g_raw[unit][:, :, half * CHUNK : (half + 1) * CHUNK].rearrange(
@@ -133,14 +141,13 @@ def tile_selfattention3d_pa_k_kernel(
                 in_=g_grouped[chunk][:].rearrange("p e r j -> p (e r j)"),
             )
 
-        def transpose_w(job):
+        def transpose_w(job, banks):
             if job >= EARLY_JOBS + LATE_JOBS:
                 return
             pairs = w_raw[job][:].bitcast(F32)
-            w_banks[job] = []
-            for k in range(4):
+            for k in banks:
                 bank = work.tile([P, 4, P], F32, name="work")
-                w_banks[job].append(bank)
+                w_banks[(job, k)] = bank
                 for i in range(2):
                     if job < EARLY_JOBS:
                         first = ((k % 2) * 2 + i) * (UNIT // 2) + (k // 2) * (CHUNK // 2)
@@ -153,19 +160,19 @@ def tile_selfattention3d_pa_k_kernel(
                             ident_f32[:],
                         )
 
-        def empty_w_banks(job):
+        def empty_w_banks(job, banks):
             if job >= EARLY_JOBS + LATE_JOBS:
                 return
-            for k in range(4):
+            for k in banks:
                 if k % 2 == 0:
                     w_grouped[(job, k // 2)] = grouped.tile(
-                        [P, 4 * CHUNK], BF16, name="w_grouped", align_bytes=64, bufs=2 * LATE_JOBS_FIRST + 1
+                        [P, 4 * CHUNK], BF16, name="w_grouped", align_bytes=64, bufs=3
                     )
                 target = w_grouped[(job, k // 2)][:].bitcast(F32).rearrange(
                     "p (k i c h) -> p k i c h", k=2, i=2, h=2
                 )[:, k % 2]
-                source = w_banks[job][k][:].rearrange("p (i h) c -> p i c h", h=2)
-                if job >= EARLY_JOBS + LATE_JOBS_FIRST and k % 2 == 1 or job < EARLY_JOBS and k == 3:
+                source = w_banks[(job, k)][:].rearrange("p (i h) c -> p i c h", h=2)
+                if job >= EARLY_JOBS and k % 2 == 1 or 2 < job < EARLY_JOBS and job % 2 == 1 and k == 3:
                     nc.vector.tensor_copy(out=target, in_=source)
                 else:
                     nc.scalar.copy(out=target, in_=source)
@@ -254,24 +261,17 @@ def tile_selfattention3d_pa_k_kernel(
             )
             nc.sync.dma_start(out=out_rows[:, i, :], in_=out_sb[:])
 
-        job_order = (
-            list(range(EARLY_JOBS, EARLY_JOBS + LATE_JOBS_FIRST))
-            + list(range(EARLY_JOBS))
-            + list(range(EARLY_JOBS + LATE_JOBS_FIRST, EARLY_JOBS + LATE_JOBS))
-        )
-
-        def load_w_at(place):
-            if place < len(job_order):
-                load_w(job_order[place])
-
         theta_sb = keep.tile([P, N_Q // P, C1], BF16)
         phi_sb = keep.tile([P, PACK, C1], BF16)
         nc.sync.dma_start(out=phi_sb[:], in_=phi_rows)
         nc.sync.dma_start(out=theta_sb[:], in_=theta_rows)
-        load_g(0, pieces=2)
-        for place in range(RAW_BUFS):
-            load_w_at(place)
+        load_g(0, 0, 2)
+        load_g(0, 1, 2)
+        load_w(0)
+        load_w(1)
         load_g(1)
+        load_w(2)
+        load_g(2)
 
         make_identity(nc, ident_bf16[:])
         make_identity(nc, ident_f32[:])
@@ -290,6 +290,7 @@ def tile_selfattention3d_pa_k_kernel(
         nc.scalar.copy(out=theta_t[:], in_=theta_bank[:].rearrange("c a p -> c (a p)"))
 
         regroup_g(0)
+        regroup_g(1, on_gpsimd=True)
 
         minus_peak = keep.tile([P, PACK], F32)
         total = keep.tile([P, PACK], F32)
@@ -309,12 +310,9 @@ def tile_selfattention3d_pa_k_kernel(
                 scale=-1.0,
                 accum_out=total[:, j : j + 1],
             )
-        for place in range(LATE_JOBS_FIRST):
-            transpose_w(job_order[place])
-            load_w_at(place + RAW_BUFS)
-            empty_w_banks(job_order[place])
-            if place == 0:
-                load_g(2)
+        transpose_w(0, range(4))
+        load_w(3)
+        empty_w_banks(0, range(4))
 
         attn_grouped = keep.tile([P, N_Q, PACK], BF16, align_bytes=64)
 
@@ -344,71 +342,89 @@ def tile_selfattention3d_pa_k_kernel(
         quantise_attn(1)
         normalise(3)
         quantise_attn(2)
-        regroup_g(1)
-        load_g(RAW_BUFS)
         quantise_attn(3)
         quantise_g(1)
-        for place in range(LATE_JOBS_FIRST):
-            quantise_w(job_order[place], 0)
-            quantise_w(job_order[place], 1)
+        regroup_g(2)
+        quantise_w(0, 0)
+        quantise_w(0, 1)
 
         y_early = []
         for i in range(EARLY_TILES):
             y_early.append(y_banks.tile([P, N_Q], F32, name="y%d" % i))
 
-        for k in range(N_UNITS):
-            regroup_g(2 * k + 2)
-            quantise_a(2 * k - 1)
-            regroup_g(2 * k + 3)
-            load_g(k + 1 + RAW_BUFS)
-            quantise_g(2 * k + 2)
-            for half in range(2):
-                for b in range(PACK):
-                    make_a(2 * k + half, b)
-                    if k > 0:
-                        project_early(y_early[b], b, 2 * k - 2 + half)
-                if half == 0:
-                    quantise_a(2 * k)
-                    transpose_w(k)
-                    load_w_at(LATE_JOBS_FIRST + k + RAW_BUFS)
-                    empty_w_banks(k)
-                    quantise_g(2 * k + 3)
-                    quantise_w(k, 0)
-                    quantise_w(k, 1)
-            if k == 0:
+        def project_some(chunk, tiles):
+            if chunk >= 0:
+                for i in tiles:
+                    project_early(y_early[i], i, chunk)
+
+        for c in range(N_CHUNKS):
+            job = c // 2 + 1
+            if c % 2 == 0:
+                if c > 0:
+                    regroup_g(c + 2)
+                quantise_a(c - 1)
+                regroup_g(c + 3)
+                quantise_g(c + 2)
+            for b in range(PACK):
+                make_a(c, b)
+                project_some(c - 2, (b,))
+            if c % 2 == 0:
+                quantise_a(c)
+                transpose_w(job, range(4))
+                load_g(c // 2 + 3)
+                load_w(c // 2 + 4)
+                empty_w_banks(job, range(4))
+                quantise_g(c + 3)
+                quantise_w(job, 0)
+                quantise_w(job, 1)
+            if c == 1:
                 bias_rows = keep.tile([P, P], BF16)
                 nc.vector.memset(bias_rows[:], 0.0)
                 gamma_sb = keep.tile([P, 1], BF16)
                 nc.sync.dma_start(out=bias_rows[0:N_TILES, :], in_=b_attn_g.rearrange("(i c) -> i c", c=P))
                 nc.sync.dma_start(out=gamma_sb[:], in_=gamma.partition_broadcast(P))
                 nc.sync.dma_start(out=x_sb[:], in_=x_rows)
+            if c == 5:
+                bias_bank = work.tile([P, P], BF16, name="work")
+                nc.tensor.transpose(bias_bank[:], bias_rows[:], ident_bf16[:])
+                nc.vector.tensor_copy(out=bias_col[:], in_=bias_bank[:, 0:N_TILES])
+                exp_minus_gamma = keep.tile([P, 1], F32)
+                nc.scalar.activation(out=exp_minus_gamma[:], in_=gamma_sb[:], func=ACT.Exp, scale=-1.0)
+                nc.vector.tensor_scalar_add(exp_minus_gamma[:], exp_minus_gamma[:], 1.0)
+                nc.vector.reciprocal(alpha[:], exp_minus_gamma[:])
+                nc.vector.tensor_scalar(
+                    out=one_minus_alpha[:], in0=alpha[:], scalar1=-1.0, scalar2=1.0, op0=ALU.mult, op1=ALU.add
+                )
 
         quantise_a(N_CHUNKS - 1)
-        for i in range(EARLY_TILES):
-            project_early(y_early[i], i, N_CHUNKS - 2)
+        job = EARLY_JOBS + 1
+        project_some(N_CHUNKS - 2, range(EARLY_TILES))
+        transpose_w(job, range(4))
+        empty_w_banks(job, range(4))
+        quantise_w(job, 0)
+        quantise_w(job, 1)
+        project_some(N_CHUNKS - 1, range(EARLY_TILES))
 
-        bias_bank = work.tile([P, P], BF16, name="work")
-        nc.tensor.transpose(bias_bank[:], bias_rows[:], ident_bf16[:])
-        nc.vector.tensor_copy(out=bias_col[:], in_=bias_bank[:, 0:N_TILES])
-        exp_minus_gamma = keep.tile([P, 1], F32)
-        nc.scalar.activation(out=exp_minus_gamma[:], in_=gamma_sb[:], func=ACT.Exp, scale=-1.0)
-        nc.vector.tensor_scalar_add(exp_minus_gamma[:], exp_minus_gamma[:], 1.0)
-        nc.vector.reciprocal(alpha[:], exp_minus_gamma[:])
-        nc.vector.tensor_scalar(
-            out=one_minus_alpha[:], in0=alpha[:], scalar1=-1.0, scalar2=1.0, op0=ALU.mult, op1=ALU.add
-        )
-
-        for job in range(EARLY_JOBS + LATE_JOBS_FIRST, EARLY_JOBS + LATE_JOBS):
-            transpose_w(job)
-            empty_w_banks(job)
-            quantise_w(job, 0)
-            quantise_w(job, 1)
-        for i in range(EARLY_TILES):
-            project_early(y_early[i], i, N_CHUNKS - 1)
-        for i in range(EARLY_TILES):
+        quarter = N_CHUNKS // 4
+        y_late = {}
+        for i in range(2):
             finish(y_early[i], i)
-        for i in range(EARLY_TILES, N_TILES):
-            y_late = work.tile([P, N_Q], F32, name="work")
-            for chunk in range(N_CHUNKS):
-                project_late(y_late, i, chunk)
-            finish(y_late, i)
+            y_late[EARLY_TILES + i] = y_banks.tile([P, N_Q], F32, name="y%d" % i)
+        for q in range(4):
+            job = EARLY_JOBS + 2 + q
+            if q < 2:
+                transpose_w(job, range(4))
+                empty_w_banks(job, range(4))
+                quantise_w(job, 0)
+                quantise_w(job, 1)
+                finish(y_early[2 + q], 2 + q)
+            for chunk in range(q * quarter, (q + 1) * quarter):
+                project_late(y_late[EARLY_TILES], EARLY_TILES, chunk)
+            if q == 3:
+                finish(y_late[EARLY_TILES], EARLY_TILES)
+            if q < 2:
+                for chunk in range(q * quarter, (q + 1) * quarter):
+                    project_late(y_late[EARLY_TILES + 1], EARLY_TILES + 1, chunk)
+        for chunk in range(2 * quarter, 4 * quarter):
+            project_late(y_late[EARLY_TILES + 1], EARLY_TILES + 1, chunk)
+        finish(y_late[EARLY_TILES + 1], EARLY_TILES + 1)

@@ -28,6 +28,7 @@ LATE_TILES = N_TILES - EARLY_TILES
 WORK_BANKS = 8 - EARLY_TILES
 EARLY_JOBS = N_UNITS
 LATE_JOBS = LATE_TILES * C2 // (4 * UNIT)
+GATE_CHUNK = 5
 RAW_BUFS = 3
 
 FLOPS = 2 * N_Q * N_K * C1 + 2 * N_Q * N_K * C2 + 2 * CH * C2 * N_Q
@@ -226,13 +227,13 @@ def tile_selfattention3d_pa_k_kernel(
                 in_=a_grouped[chunk][:].rearrange("p n t -> p (n t)"),
             )
 
-        def project(y, words, scales, chunk):
+        def project(y, words, scales, chunk, queries=slice(0, N_Q)):
             nc.tensor.matmul_mx(
                 out=y[:],
                 lhsT=words.bitcast(FP8X4),
                 lhsT_scale=scales,
-                rhs=a_codes[:, chunk, :].bitcast(FP8X4),
-                rhs_scale=a_scales[:, chunk, :],
+                rhs=a_codes[:, chunk, queries].bitcast(FP8X4),
+                rhs_scale=a_scales[:, chunk, queries],
                 start=(chunk == 0),
                 stop=(chunk == N_CHUNKS - 1),
             )
@@ -242,24 +243,36 @@ def tile_selfattention3d_pa_k_kernel(
             columns = slice(i * P, (i + 1) * P)
             project(y, words[:, chunk % 2, columns], scales[:, chunk % 2, columns], chunk)
 
-        def project_late(y, i, chunk):
+        def project_late(y, i, chunk, queries=slice(0, N_Q)):
             first = (chunk % 2) * LATE_TILES * P + (i - EARLY_TILES) * P
             columns = slice(first, first + P)
-            project(y, late_codes[:, chunk // 2, columns], late_scales[:, chunk // 2, columns], chunk)
+            project(y, late_codes[:, chunk // 2, columns], late_scales[:, chunk // 2, columns], chunk, queries)
 
-        def finish(y, i):
+        def finish(y, i, queries=slice(0, N_Q)):
+            width = queries.stop - queries.start
             attn_g_sb = results.tile([P, N_Q], F32, name="attn_g_sb")
-            nc.scalar.activation(out=attn_g_sb[:], in_=y[:], func=ACT.Identity, bias=bias_col[:, i : i + 1])
-            nc.sync.dma_start(out=attn_g_rows[:, i, :], in_=attn_g_sb[:])
+            nc.scalar.activation(
+                out=attn_g_sb[:, 0:width], in_=y[:], func=ACT.Identity, bias=bias_col[:, i : i + 1]
+            )
+            nc.sync.dma_start(out=attn_g_rows[:, i, queries], in_=attn_g_sb[:, 0:width])
             x_part = results.tile([P, N_Q], F32, name="x_part")
             nc.vector.tensor_scalar(
-                out=x_part[:], in0=x_sb[:, i, :], scalar1=one_minus_alpha[:, 0:1], scalar2=None, op0=ALU.mult
+                out=x_part[:, 0:width],
+                in0=x_sb[:, i, queries],
+                scalar1=one_minus_alpha[:, 0:1],
+                scalar2=None,
+                op0=ALU.mult,
             )
             out_sb = results.tile([P, N_Q], F32, name="out_sb")
             nc.vector.scalar_tensor_tensor(
-                out=out_sb[:], in0=attn_g_sb[:], scalar=alpha[:, 0:1], in1=x_part[:], op0=ALU.mult, op1=ALU.add
+                out=out_sb[:, 0:width],
+                in0=attn_g_sb[:, 0:width],
+                scalar=alpha[:, 0:1],
+                in1=x_part[:, 0:width],
+                op0=ALU.mult,
+                op1=ALU.add,
             )
-            nc.sync.dma_start(out=out_rows[:, i, :], in_=out_sb[:])
+            nc.sync.dma_start(out=out_rows[:, i, queries], in_=out_sb[:, 0:width])
 
         theta_sb = keep.tile([P, N_Q // P, C1], BF16)
         phi_sb = keep.tile([P, PACK, C1], BF16)
@@ -270,6 +283,9 @@ def tile_selfattention3d_pa_k_kernel(
         load_w(0)
         load_w(1)
         load_g(1)
+        bias_rows = keep.tile([P, P], BF16)
+        nc.vector.memset(bias_rows[:], 0.0)
+        nc.sync.dma_start(out=bias_rows[0:N_TILES, :], in_=b_attn_g.rearrange("(i c) -> i c", c=P))
         load_w(2)
         load_g(2)
 
@@ -349,8 +365,6 @@ def tile_selfattention3d_pa_k_kernel(
         quantise_w(0, 1)
 
         y_early = []
-        for i in range(EARLY_TILES):
-            y_early.append(y_banks.tile([P, N_Q], F32, name="y%d" % i))
 
         def project_some(chunk, tiles):
             if chunk >= 0:
@@ -366,8 +380,15 @@ def tile_selfattention3d_pa_k_kernel(
                 regroup_g(c + 3)
                 quantise_g(c + 2)
             for b in range(PACK):
-                make_a(c, b)
                 project_some(c - 2, (b,))
+                make_a(c, b)
+            if c == 0:
+                bias_bank = y_banks.tile([P, P], BF16, name="y3")
+                nc.tensor.transpose(bias_bank[:], bias_rows[:], ident_bf16[:])
+                nc.vector.tensor_copy(out=bias_col[:], in_=bias_bank[:, 0:N_TILES])
+            if c == 1:
+                for i in range(EARLY_TILES):
+                    y_early.append(y_banks.tile([P, N_Q], F32, name="y%d" % i))
             if c % 2 == 0:
                 quantise_a(c)
                 transpose_w(job, range(4))
@@ -377,17 +398,11 @@ def tile_selfattention3d_pa_k_kernel(
                 quantise_g(c + 3)
                 quantise_w(job, 0)
                 quantise_w(job, 1)
-            if c == 1:
-                bias_rows = keep.tile([P, P], BF16)
-                nc.vector.memset(bias_rows[:], 0.0)
+            if c == GATE_CHUNK:
                 gamma_sb = keep.tile([P, 1], BF16)
-                nc.sync.dma_start(out=bias_rows[0:N_TILES, :], in_=b_attn_g.rearrange("(i c) -> i c", c=P))
                 nc.sync.dma_start(out=gamma_sb[:], in_=gamma.partition_broadcast(P))
                 nc.sync.dma_start(out=x_sb[:], in_=x_rows)
-            if c == 5:
-                bias_bank = work.tile([P, P], BF16, name="work")
-                nc.tensor.transpose(bias_bank[:], bias_rows[:], ident_bf16[:])
-                nc.vector.tensor_copy(out=bias_col[:], in_=bias_bank[:, 0:N_TILES])
+            if c == GATE_CHUNK + 4:
                 exp_minus_gamma = keep.tile([P, 1], F32)
                 nc.scalar.activation(out=exp_minus_gamma[:], in_=gamma_sb[:], func=ACT.Exp, scale=-1.0)
                 nc.vector.tensor_scalar_add(exp_minus_gamma[:], exp_minus_gamma[:], 1.0)
@@ -406,25 +421,30 @@ def tile_selfattention3d_pa_k_kernel(
         project_some(N_CHUNKS - 1, range(EARLY_TILES))
 
         quarter = N_CHUNKS // 4
-        y_late = {}
+        first, last = EARLY_TILES, EARLY_TILES + 1
+        halves = (slice(0, N_Q // 2), slice(N_Q // 2, N_Q))
         for i in range(2):
             finish(y_early[i], i)
-            y_late[EARLY_TILES + i] = y_banks.tile([P, N_Q], F32, name="y%d" % i)
-        for q in range(4):
+        y_first = y_banks.tile([P, N_Q], F32, name="y0")
+        for q in range(2):
             job = EARLY_JOBS + 2 + q
-            if q < 2:
-                transpose_w(job, range(4))
-                empty_w_banks(job, range(4))
-                quantise_w(job, 0)
-                quantise_w(job, 1)
-                finish(y_early[2 + q], 2 + q)
-            for chunk in range(q * quarter, (q + 1) * quarter):
-                project_late(y_late[EARLY_TILES], EARLY_TILES, chunk)
-            if q == 3:
-                finish(y_late[EARLY_TILES], EARLY_TILES)
-            if q < 2:
-                for chunk in range(q * quarter, (q + 1) * quarter):
-                    project_late(y_late[EARLY_TILES + 1], EARLY_TILES + 1, chunk)
-        for chunk in range(2 * quarter, 4 * quarter):
-            project_late(y_late[EARLY_TILES + 1], EARLY_TILES + 1, chunk)
-        finish(y_late[EARLY_TILES + 1], EARLY_TILES + 1)
+            transpose_w(job, range(4))
+            empty_w_banks(job, range(4))
+            quantise_w(job, 0)
+            quantise_w(job, 1)
+            finish(y_early[2 + q], 2 + q)
+            for chunk in range(q * 2 * quarter, (q + 2) * quarter):
+                project_late(y_first, first, chunk)
+        y_last = []
+        for h in range(2):
+            y_last.append(y_banks.tile([P, N_Q // 2], F32, name="y%d" % (1 + h)))
+        for h in range(2):
+            for chunk in range((3 - h) * quarter):
+                project_late(y_last[h], last, chunk, halves[h])
+        for chunk in range(3 * quarter, 4 * quarter):
+            project_late(y_first, first, chunk)
+        finish(y_first, first)
+        for h in range(2):
+            for chunk in range((3 - h) * quarter, 4 * quarter):
+                project_late(y_last[h], last, chunk, halves[h])
+            finish(y_last[h], last, halves[h])

@@ -28,7 +28,7 @@ LATE_TILES = N_TILES - EARLY_TILES
 WORK_BANKS = 8 - EARLY_TILES
 EARLY_JOBS = N_UNITS
 LATE_JOBS = LATE_TILES * C2 // (4 * UNIT)
-GATE_CHUNK = 5
+GATE_CHUNK = 11
 RAW_BUFS = 3
 
 FLOPS = 2 * N_Q * N_K * C1 + 2 * N_Q * N_K * C2 + 2 * CH * C2 * N_Q
@@ -281,13 +281,13 @@ def tile_selfattention3d_pa_k_kernel(
         load_g(0, 0, 2)
         load_g(0, 1, 2)
         load_w(0)
-        load_w(1)
         load_g(1)
+        load_w(1)
         bias_rows = keep.tile([P, P], BF16)
         nc.vector.memset(bias_rows[:], 0.0)
         nc.sync.dma_start(out=bias_rows[0:N_TILES, :], in_=b_attn_g.rearrange("(i c) -> i c", c=P))
-        load_w(2)
         load_g(2)
+        load_w(2)
 
         make_identity(nc, ident_bf16[:])
         make_identity(nc, ident_f32[:])
@@ -327,7 +327,6 @@ def tile_selfattention3d_pa_k_kernel(
                 accum_out=total[:, j : j + 1],
             )
         transpose_w(0, range(4))
-        load_w(3)
         empty_w_banks(0, range(4))
 
         attn_grouped = keep.tile([P, N_Q, PACK], BF16, align_bytes=64)
@@ -362,7 +361,6 @@ def tile_selfattention3d_pa_k_kernel(
         quantise_g(1)
         regroup_g(2)
         quantise_w(0, 0)
-        quantise_w(0, 1)
 
         y_early = []
 
@@ -377,8 +375,8 @@ def tile_selfattention3d_pa_k_kernel(
                 if c > 0:
                     regroup_g(c + 2)
                 quantise_a(c - 1)
-                regroup_g(c + 3)
                 quantise_g(c + 2)
+                regroup_g(c + 3)
             for b in range(PACK):
                 project_some(c - 2, (b,))
                 make_a(c, b)
@@ -391,9 +389,14 @@ def tile_selfattention3d_pa_k_kernel(
                     y_early.append(y_banks.tile([P, N_Q], F32, name="y%d" % i))
             if c % 2 == 0:
                 quantise_a(c)
-                transpose_w(job, range(4))
+                if c == 0:
+                    quantise_w(0, 1)
                 load_g(c // 2 + 3)
-                load_w(c // 2 + 4)
+                if c // 2 + 3 <= N_UNITS:
+                    load_w(c // 2 + 3)
+                transpose_w(job, range(4))
+                if c // 2 + 3 >= N_UNITS:
+                    load_w(c // 2 + 4)
                 empty_w_banks(job, range(4))
                 quantise_g(c + 3)
                 quantise_w(job, 0)

@@ -28,7 +28,7 @@ LATE_TILES = N_TILES - EARLY_TILES
 WORK_BANKS = 8 - EARLY_TILES
 EARLY_JOBS = N_UNITS
 LATE_JOBS = LATE_TILES * C2 // (4 * UNIT)
-GATE_CHUNK = 11
+GATE_CHUNK = 9
 RAW_BUFS = 3
 
 FLOPS = 2 * N_Q * N_K * C1 + 2 * N_Q * N_K * C2 + 2 * CH * C2 * N_Q
@@ -60,8 +60,8 @@ def tile_selfattention3d_pa_k_kernel(
         attn_scales = keep.tile([P, N_Q], U8, align_bytes=64)
         a_codes = keep.tile([P, N_CHUNKS, N_Q], U32, align_bytes=64)
         a_scales = keep.tile([P, N_CHUNKS, N_Q], U8, align_bytes=64)
-        late_codes = keep.tile([P, 2 * LATE_JOBS, CHUNK], U32, align_bytes=64)
-        late_scales = keep.tile([P, 2 * LATE_JOBS, CHUNK], U8, align_bytes=64)
+        late_codes = keep.tile([P, 4 * LATE_TILES, CHUNK], U32, align_bytes=64)
+        late_scales = keep.tile([P, 4 * LATE_TILES, CHUNK], U8, align_bytes=64)
         ident_bf16 = keep.tile([P, P], BF16)
         ident_f32 = keep.tile([P, P], F32)
         x_sb = keep.tile([P, N_TILES, N_Q], BF16)
@@ -77,6 +77,8 @@ def tile_selfattention3d_pa_k_kernel(
         w_banks = {}
         w_grouped = {}
         w_codes = {}
+        x_parts = {}
+        attn_gs = {}
 
         def load_g(unit, piece=0, pieces=1):
             if unit >= N_UNITS:
@@ -99,11 +101,9 @@ def tile_selfattention3d_pa_k_kernel(
                     in_=w_rows[:, 0:EARLY_TILES, job * UNIT : (job + 1) * UNIT],
                 )
             else:
-                first = (job - EARLY_JOBS) * 2 * UNIT
-                nc.sync.dma_start(
-                    out=w_raw[job][:].rearrange("p (i c) -> p i c", i=LATE_TILES),
-                    in_=w_rows[:, EARLY_TILES:N_TILES, first : first + 2 * UNIT],
-                )
+                tile, part = divmod(job - EARLY_JOBS, 2)
+                first = part * 4 * UNIT
+                nc.sync.dma_start(out=w_raw[job][:], in_=w_rows[:, EARLY_TILES + tile, first : first + 4 * UNIT])
 
         def regroup_g(chunk, on_gpsimd=False):
             if chunk >= N_CHUNKS:
@@ -153,7 +153,7 @@ def tile_selfattention3d_pa_k_kernel(
                     if job < EARLY_JOBS:
                         first = ((k % 2) * 2 + i) * (UNIT // 2) + (k // 2) * (CHUNK // 2)
                     else:
-                        first = i * UNIT + k * (CHUNK // 2)
+                        first = (2 * k + i) * (CHUNK // 2)
                     for h in range(2):
                         nc.tensor.transpose(
                             bank[:, 2 * i + h, :],
@@ -167,13 +167,13 @@ def tile_selfattention3d_pa_k_kernel(
             for k in banks:
                 if k % 2 == 0:
                     w_grouped[(job, k // 2)] = grouped.tile(
-                        [P, 4 * CHUNK], BF16, name="w_grouped", align_bytes=64, bufs=3
+                        [P, 4 * CHUNK], BF16, name="w_grouped", align_bytes=64, bufs=4
                     )
                 target = w_grouped[(job, k // 2)][:].bitcast(F32).rearrange(
                     "p (k i c h) -> p k i c h", k=2, i=2, h=2
                 )[:, k % 2]
                 source = w_banks[(job, k)][:].rearrange("p (i h) c -> p i c h", h=2)
-                if job >= EARLY_JOBS and k % 2 == 1 or 2 < job < EARLY_JOBS and job % 2 == 1 and k == 3:
+                if 2 < job < EARLY_JOBS and job % 2 == 1 and k == 3 or job > EARLY_JOBS and k % 2 == 1:
                     nc.vector.tensor_copy(out=target, in_=source)
                 else:
                     nc.scalar.copy(out=target, in_=source)
@@ -244,31 +244,35 @@ def tile_selfattention3d_pa_k_kernel(
             project(y, words[:, chunk % 2, columns], scales[:, chunk % 2, columns], chunk)
 
         def project_late(y, i, chunk, queries=slice(0, N_Q)):
-            first = (chunk % 2) * LATE_TILES * P + (i - EARLY_TILES) * P
-            columns = slice(first, first + P)
-            project(y, late_codes[:, chunk // 2, columns], late_scales[:, chunk // 2, columns], chunk, queries)
+            slot = 4 * (i - EARLY_TILES) + chunk // 4
+            columns = slice((chunk % 4) * P, (chunk % 4 + 1) * P)
+            project(y, late_codes[:, slot, columns], late_scales[:, slot, columns], chunk, queries)
 
-        def finish(y, i, queries=slice(0, N_Q)):
+        def weigh_x(i, queries=slice(0, N_Q)):
+            width = queries.stop - queries.start
+            x_part = results.tile([P, N_Q], F32, name="x_part")
+            nc.scalar.activation(
+                out=x_part[:, 0:width], in_=x_sb[:, i, queries], func=ACT.Copy, scale=one_minus_alpha[:, 0:1]
+            )
+            x_parts[(i, queries.start)] = x_part
+
+        def store_attn_g(y, i, queries=slice(0, N_Q)):
             width = queries.stop - queries.start
             attn_g_sb = results.tile([P, N_Q], F32, name="attn_g_sb")
             nc.scalar.activation(
                 out=attn_g_sb[:, 0:width], in_=y[:], func=ACT.Identity, bias=bias_col[:, i : i + 1]
             )
             nc.sync.dma_start(out=attn_g_rows[:, i, queries], in_=attn_g_sb[:, 0:width])
-            x_part = results.tile([P, N_Q], F32, name="x_part")
-            nc.vector.tensor_scalar(
-                out=x_part[:, 0:width],
-                in0=x_sb[:, i, queries],
-                scalar1=one_minus_alpha[:, 0:1],
-                scalar2=None,
-                op0=ALU.mult,
-            )
+            attn_gs[(i, queries.start)] = attn_g_sb
+
+        def store_out(i, queries=slice(0, N_Q)):
+            width = queries.stop - queries.start
             out_sb = results.tile([P, N_Q], F32, name="out_sb")
             nc.vector.scalar_tensor_tensor(
                 out=out_sb[:, 0:width],
-                in0=attn_g_sb[:, 0:width],
+                in0=attn_gs[(i, queries.start)][:, 0:width],
                 scalar=alpha[:, 0:1],
-                in1=x_part[:, 0:width],
+                in1=x_parts[(i, queries.start)][:, 0:width],
                 op0=ALU.mult,
                 op1=ALU.add,
             )
@@ -404,8 +408,8 @@ def tile_selfattention3d_pa_k_kernel(
             if c == GATE_CHUNK:
                 gamma_sb = keep.tile([P, 1], BF16)
                 nc.sync.dma_start(out=gamma_sb[:], in_=gamma.partition_broadcast(P))
-                nc.sync.dma_start(out=x_sb[:], in_=x_rows)
             if c == GATE_CHUNK + 4:
+                nc.sync.dma_start(out=x_sb[:], in_=x_rows)
                 exp_minus_gamma = keep.tile([P, 1], F32)
                 nc.scalar.activation(out=exp_minus_gamma[:], in_=gamma_sb[:], func=ACT.Exp, scale=-1.0)
                 nc.vector.tensor_scalar_add(exp_minus_gamma[:], exp_minus_gamma[:], 1.0)
@@ -414,40 +418,50 @@ def tile_selfattention3d_pa_k_kernel(
                     out=one_minus_alpha[:], in0=alpha[:], scalar1=-1.0, scalar2=1.0, op0=ALU.mult, op1=ALU.add
                 )
 
-        quantise_a(N_CHUNKS - 1)
-        job = EARLY_JOBS + 1
-        project_some(N_CHUNKS - 2, range(EARLY_TILES))
-        transpose_w(job, range(4))
-        empty_w_banks(job, range(4))
-        quantise_w(job, 0)
-        quantise_w(job, 1)
-        project_some(N_CHUNKS - 1, range(EARLY_TILES))
-
-        quarter = N_CHUNKS // 4
         first, last = EARLY_TILES, EARLY_TILES + 1
+        middle = N_CHUNKS // 2
         halves = (slice(0, N_Q // 2), slice(N_Q // 2, N_Q))
-        for i in range(2):
-            finish(y_early[i], i)
+        quantise_a(N_CHUNKS - 1)
+        project_some(N_CHUNKS - 2, range(EARLY_TILES))
+        transpose_w(EARLY_JOBS + 1, range(4))
+        empty_w_banks(EARLY_JOBS + 1, range(4))
+        project_some(N_CHUNKS - 1, range(EARLY_TILES))
+        quantise_w(EARLY_JOBS + 1, 0)
+        quantise_w(EARLY_JOBS + 1, 1)
+        for i in range(3):
+            store_attn_g(y_early[i], i)
+        transpose_w(EARLY_JOBS + 2, range(4))
+        empty_w_banks(EARLY_JOBS + 2, range(4))
+        weigh_x(0)
+        store_out(0)
+        quantise_w(EARLY_JOBS + 2, 0)
+        weigh_x(1)
+        store_out(1)
+        quantise_w(EARLY_JOBS + 2, 1)
         y_first = y_banks.tile([P, N_Q], F32, name="y0")
-        for q in range(2):
-            job = EARLY_JOBS + 2 + q
-            transpose_w(job, range(4))
-            empty_w_banks(job, range(4))
-            quantise_w(job, 0)
-            quantise_w(job, 1)
-            finish(y_early[2 + q], 2 + q)
-            for chunk in range(q * 2 * quarter, (q + 2) * quarter):
-                project_late(y_first, first, chunk)
         y_last = []
         for h in range(2):
             y_last.append(y_banks.tile([P, N_Q // 2], F32, name="y%d" % (1 + h)))
-        for h in range(2):
-            for chunk in range((3 - h) * quarter):
-                project_late(y_last[h], last, chunk, halves[h])
-        for chunk in range(3 * quarter, 4 * quarter):
+        for chunk in range(middle):
             project_late(y_first, first, chunk)
-        finish(y_first, first)
+        transpose_w(EARLY_JOBS + 3, range(4))
+        empty_w_banks(EARLY_JOBS + 3, range(4))
+        quantise_w(EARLY_JOBS + 3, 0)
+        weigh_x(2)
+        store_out(2)
+        quantise_w(EARLY_JOBS + 3, 1)
+        store_attn_g(y_early[3], 3)
+        weigh_x(3)
+        store_out(3)
+        for chunk in range(middle, N_CHUNKS):
+            project_late(y_first, first, chunk)
+        store_attn_g(y_first, first)
+        weigh_x(first)
+        store_out(first)
         for h in range(2):
-            for chunk in range((3 - h) * quarter, 4 * quarter):
+            weigh_x(last, halves[h])
+        for h in range(2):
+            for chunk in range(N_CHUNKS):
                 project_late(y_last[h], last, chunk, halves[h])
-            finish(y_last[h], last, halves[h])
+            store_attn_g(y_last[h], last, halves[h])
+            store_out(last, halves[h])

from contextlib import ExitStack

import concourse.mybir as mybir
from concourse.masks import make_identity

F32 = mybir.dt.float32
BF16 = mybir.dt.bfloat16
U32 = mybir.dt.uint32
U8 = mybir.dt.uint8
FP8X4 = mybir.dt.float8_e4m3fn_x4
ACT = mybir.ActivationFunctionType
ALU = mybir.AluOpType

P = 128
PACK = 4
N_Q = 512
N_K = 512
C1 = 128
C2 = 8192
CH = 768
CHUNK = P * PACK
N_CHUNKS = C2 // CHUNK
UNIT = 2 * CHUNK
N_UNITS = C2 // UNIT
N_TILES = CH // P
EARLY_TILES = 4
LATE_TILES = N_TILES - EARLY_TILES
WORK_BANKS = 8 - EARLY_TILES
EARLY_JOBS = N_UNITS
LATE_JOBS = LATE_TILES * C2 // (4 * UNIT)
GATE_CHUNK = 9
RAW_BUFS = 3

FLOPS = 2 * N_Q * N_K * C1 + 2 * N_Q * N_K * C2 + 2 * CH * C2 * N_Q


def tile_selfattention3d_pa_k_kernel(
    tc, theta, phi, g, x, w_attn_g, b_attn_g, gamma, out_0, out_1
):
    nc = tc.nc
    with ExitStack() as ctx:
        ctx.enter_context(tc.manual_schedule())
        keep = ctx.enter_context(tc.tile_pool(name="keep", bufs=1))
        raw = ctx.enter_context(tc.tile_pool(name="raw", bufs=RAW_BUFS))
        grouped = ctx.enter_context(tc.tile_pool(name="grouped", bufs=3))
        codes = ctx.enter_context(tc.tile_pool(name="codes", bufs=3))
        results = ctx.enter_context(tc.tile_pool(name="results", bufs=3))
        y_banks = ctx.enter_context(tc.psum_pool(name="y_banks", bufs=1))
        work = ctx.enter_context(tc.psum_pool(name="work", bufs=WORK_BANKS))

        theta_rows = theta.rearrange("b (a p) c -> p (b a) c", p=P)
        phi_rows = phi.rearrange("b (p j) c -> p (b j) c", j=PACK)
        g_rows = g.rearrange("b (p j) c -> p (b j) c", j=PACK)
        w_rows = w_attn_g.rearrange("(i p) c -> p i c", p=P)
        x_rows = x.rearrange("b (i p) f r c -> p (b i) (f r c)", p=P)
        out_rows = out_0.rearrange("b (i p) f r c -> p (b i) (f r c)", p=P)
        attn_g_rows = out_1.rearrange("b (i p) f r c -> p (b i) (f r c)", p=P)

        attn_codes = keep.tile([P, N_Q], U32, align_bytes=64)
        attn_scales = keep.tile([P, N_Q], U8, align_bytes=64)
        a_codes = keep.tile([P, N_CHUNKS, N_Q], U32, align_bytes=64)
        a_scales = keep.tile([P, N_CHUNKS, N_Q], U8, align_bytes=64)
        late_codes = keep.tile([P, 4 * LATE_TILES, CHUNK], U32, align_bytes=64)
        late_scales = keep.tile([P, 4 * LATE_TILES, CHUNK], U8, align_bytes=64)
        ident_bf16 = keep.tile([P, P], BF16)
        ident_f32 = keep.tile([P, P], F32)
        x_sb = keep.tile([P, N_TILES, N_Q], BF16)
        bias_col = keep.tile([P, N_TILES], F32)
        alpha = keep.tile([P, 1], F32)
        one_minus_alpha = keep.tile([P, 1], F32)

        g_raw = {}
        w_raw = {}
        g_grouped = {}
        g_codes = {}
        a_grouped = {}
        w_banks = {}
        w_grouped = {}
        w_codes = {}
        x_parts = {}
        attn_gs = {}

        def load_g(unit, piece=0, pieces=1):
            if unit >= N_UNITS:
                return
            if piece == 0:
                g_raw[unit] = raw.tile([P, PACK, UNIT], BF16, name="g_raw")
            width = UNIT // pieces
            nc.sync.dma_start(
                out=g_raw[unit][:, :, piece * width : (piece + 1) * width],
                in_=g_rows[:, :, unit * UNIT + piece * width : unit * UNIT + (piece + 1) * width],
            )

        def load_w(job):
            if job >= EARLY_JOBS + LATE_JOBS:
                return
            w_raw[job] = raw.tile([P, 4 * UNIT], BF16, name="w_raw")
            if job < EARLY_JOBS:
                nc.sync.dma_start(
                    out=w_raw[job][:].rearrange("p (i c) -> p i c", i=EARLY_TILES),
                    in_=w_rows[:, 0:EARLY_TILES, job * UNIT : (job + 1) * UNIT],
                )
            else:
                tile, part = divmod(job - EARLY_JOBS, 2)
                first = part * 4 * UNIT
                nc.sync.dma_start(out=w_raw[job][:], in_=w_rows[:, EARLY_TILES + tile, first : first + 4 * UNIT])

        def regroup_g(chunk, on_gpsimd=False):
            if chunk >= N_CHUNKS:
                return
            unit, half = divmod(chunk, 2)
            g_grouped[chunk] = grouped.tile([P, 2, CHUNK // 2, PACK], BF16, name="g_grouped", align_bytes=64)
            if on_gpsimd:
                nc.gpsimd.tensor_scalar(
                    out=g_grouped[chunk][:],
                    in0=g_raw[unit][:, :, half * CHUNK : (half + 1) * CHUNK].rearrange("p j (c e) -> p e c j", e=2),
                    scalar1=1.0,
                    scalar2=0.0,
                    op0=ALU.mult,
                    op1=ALU.add,
                )
                return
            nc.vector.tensor_copy(
                out=g_grouped[chunk][:].rearrange("p e (c i) j -> p e c j i", i=4),
                in_=g_raw[unit][:, :, half * CHUNK : (half + 1) * CHUNK].rearrange(
                    "p j (c i e) -> p e c j i", i=4, e=2
                ),
            )

        def quantise_g(chunk):
            if chunk >= N_CHUNKS:
                return
            unit, half = divmod(chunk, 2)
            if half == 0:
                words = codes.tile([P, 2, CHUNK], U32, name="g_words", align_bytes=64)
                scales = codes.tile([P, 2, CHUNK], U8, name="g_scales", align_bytes=64)
                g_codes[unit] = (words, scales)
            words, scales = g_codes[unit]
            nc.vector.quantize_mx(
                out=words[:, half, :].bitcast(FP8X4),
                scales=scales[:, half, :],
                in_=g_grouped[chunk][:].rearrange("p e r j -> p (e r j)"),
            )

        def transpose_w(job, banks):
            if job >= EARLY_JOBS + LATE_JOBS:
                return
            pairs = w_raw[job][:].bitcast(F32)
            for k in banks:
                bank = work.tile([P, 4, P], F32, name="work")
                w_banks[(job, k)] = bank
                for i in range(2):
                    if job < EARLY_JOBS:
                        first = ((k % 2) * 2 + i) * (UNIT // 2) + (k // 2) * (CHUNK // 2)
                    else:
                        first = (2 * k + i) * (CHUNK // 2)
                    for h in range(2):
                        nc.tensor.transpose(
                            bank[:, 2 * i + h, :],
                            pairs[:, first + h * P : first + (h + 1) * P],
                            ident_f32[:],
                        )

        def empty_w_banks(job, banks):
            if job >= EARLY_JOBS + LATE_JOBS:
                return
            for k in banks:
                if k % 2 == 0:
                    w_grouped[(job, k // 2)] = grouped.tile(
                        [P, 4 * CHUNK], BF16, name="w_grouped", align_bytes=64, bufs=4
                    )
                target = w_grouped[(job, k // 2)][:].bitcast(F32).rearrange(
                    "p (k i c h) -> p k i c h", k=2, i=2, h=2
                )[:, k % 2]
                source = w_banks[(job, k)][:].rearrange("p (i h) c -> p i c h", h=2)
                if 2 < job < EARLY_JOBS and job % 2 == 1 and k == 3 or job > EARLY_JOBS and k % 2 == 1:
                    nc.vector.tensor_copy(out=target, in_=source)
                else:
                    nc.scalar.copy(out=target, in_=source)

        def quantise_w(job, half):
            if job >= EARLY_JOBS + LATE_JOBS:
                return
            if job < EARLY_JOBS:
                if half == 0:
                    words = codes.tile([P, 2, CHUNK], U32, name="w_words", align_bytes=64)
                    scales = codes.tile([P, 2, CHUNK], U8, name="w_scales", align_bytes=64)
                    w_codes[job] = (words, scales)
                words, scales = w_codes[job]
                slot = half
            else:
                words, scales = late_codes, late_scales
                slot = 2 * (job - EARLY_JOBS) + half
            nc.vector.quantize_mx(
                out=words[:, slot, :].bitcast(FP8X4),
                scales=scales[:, slot, :],
                in_=w_grouped[(job, half)][:],
            )

        def make_a(chunk, block):
            unit, half = divmod(chunk, 2)
            words, scales = g_codes[unit]
            queries = slice(block * P, (block + 1) * P)
            if block == 0:
                a_grouped[chunk] = grouped.tile([P, N_Q, PACK], BF16, name="a_grouped", align_bytes=64)
            bank = work.tile([P, PACK, P], F32, name="work")
            for t in range(PACK):
                h, e = divmod(t, 2)
                columns = slice(e * (CHUNK // 2) + h * P, e * (CHUNK // 2) + (h + 1) * P)
                nc.tensor.matmul_mx(
                    out=bank[:, t, :],
                    lhsT=words[:, half, columns].bitcast(FP8X4),
                    lhsT_scale=scales[:, half, columns],
                    rhs=attn_codes[:, queries].bitcast(FP8X4),
                    rhs_scale=attn_scales[:, queries],
                    start=True,
                    stop=True,
                )
            nc.scalar.copy(out=a_grouped[chunk][:, queries, :], in_=bank[:].rearrange("p t n -> p n t"))

        def quantise_a(chunk):
            if chunk < 0 or chunk >= N_CHUNKS:
                return
            nc.vector.quantize_mx(
                out=a_codes[:, chunk, :].bitcast(FP8X4),
                scales=a_scales[:, chunk, :],
                in_=a_grouped[chunk][:].rearrange("p n t -> p (n t)"),
            )

        def project(y, words, scales, chunk, queries=slice(0, N_Q)):
            nc.tensor.matmul_mx(
                out=y[:],
                lhsT=words.bitcast(FP8X4),
                lhsT_scale=scales,
                rhs=a_codes[:, chunk, queries].bitcast(FP8X4),
                rhs_scale=a_scales[:, chunk, queries],
                start=(chunk == 0),
                stop=(chunk == N_CHUNKS - 1),
            )

        def project_early(y, i, chunk):
            words, scales = w_codes[chunk // 2]
            columns = slice(i * P, (i + 1) * P)
            project(y, words[:, chunk % 2, columns], scales[:, chunk % 2, columns], chunk)

        def project_late(y, i, chunk, queries=slice(0, N_Q)):
            slot = 4 * (i - EARLY_TILES) + chunk // 4
            columns = slice((chunk % 4) * P, (chunk % 4 + 1) * P)
            project(y, late_codes[:, slot, columns], late_scales[:, slot, columns], chunk, queries)

        def weigh_x(i, queries=slice(0, N_Q)):
            width = queries.stop - queries.start
            x_part = results.tile([P, N_Q], F32, name="x_part")
            nc.scalar.activation(
                out=x_part[:, 0:width], in_=x_sb[:, i, queries], func=ACT.Copy, scale=one_minus_alpha[:, 0:1]
            )
            x_parts[(i, queries.start)] = x_part

        def store_attn_g(y, i, queries=slice(0, N_Q)):
            width = queries.stop - queries.start
            attn_g_sb = results.tile([P, N_Q], F32, name="attn_g_sb")
            nc.scalar.activation(
                out=attn_g_sb[:, 0:width], in_=y[:], func=ACT.Identity, bias=bias_col[:, i : i + 1]
            )
            nc.sync.dma_start(out=attn_g_rows[:, i, queries], in_=attn_g_sb[:, 0:width])
            attn_gs[(i, queries.start)] = attn_g_sb

        def store_out(i, queries=slice(0, N_Q)):
            width = queries.stop - queries.start
            out_sb = results.tile([P, N_Q], F32, name="out_sb")
            nc.vector.scalar_tensor_tensor(
                out=out_sb[:, 0:width],
                in0=attn_gs[(i, queries.start)][:, 0:width],
                scalar=alpha[:, 0:1],
                in1=x_parts[(i, queries.start)][:, 0:width],
                op0=ALU.mult,
                op1=ALU.add,
            )
            nc.sync.dma_start(out=out_rows[:, i, queries], in_=out_sb[:, 0:width])

        theta_sb = keep.tile([P, N_Q // P, C1], BF16)
        phi_sb = keep.tile([P, PACK, C1], BF16)
        nc.sync.dma_start(out=phi_sb[:], in_=phi_rows)
        nc.sync.dma_start(out=theta_sb[:], in_=theta_rows)
        load_g(0, 0, 2)
        load_g(0, 1, 2)
        load_w(0)
        load_g(1)
        load_w(1)
        bias_rows = keep.tile([P, P], BF16)
        nc.vector.memset(bias_rows[:], 0.0)
        nc.sync.dma_start(out=bias_rows[0:N_TILES, :], in_=b_attn_g.rearrange("(i c) -> i c", c=P))
        load_g(2)
        load_w(2)

        make_identity(nc, ident_bf16[:])
        make_identity(nc, ident_f32[:])

        phi_bank = work.tile([P, PACK, P], BF16, name="work")
        for j in range(PACK):
            nc.tensor.transpose(phi_bank[:, j, :], phi_sb[:, j, :], ident_bf16[:])
        theta_bank = work.tile([P, N_Q // P, P], BF16, name="work")
        for a in range(N_Q // P):
            nc.tensor.transpose(theta_bank[:, a, :], theta_sb[:, a, :], ident_bf16[:])
        minus_phi_t = keep.tile([P, PACK, P], BF16)
        nc.vector.tensor_scalar(
            out=minus_phi_t[:], in0=phi_bank[:], scalar1=-1.0, scalar2=None, op0=ALU.mult
        )
        theta_t = keep.tile([P, N_Q], BF16)
        nc.scalar.copy(out=theta_t[:], in_=theta_bank[:].rearrange("c a p -> c (a p)"))

        regroup_g(0)
        regroup_g(1, on_gpsimd=True)

        minus_peak = keep.tile([P, PACK], F32)
        total = keep.tile([P, PACK], F32)
        one_over_total = keep.tile([P, PACK], F32)
        exps = keep.tile([P, PACK, N_Q], F32)
        for j in range(PACK):
            s_bank = y_banks.tile([P, N_Q], F32, name="y%d" % j)
            nc.tensor.matmul(out=s_bank[:], lhsT=minus_phi_t[:, j, :], rhs=theta_t[:], start=True, stop=True)
            nc.vector.tensor_reduce(
                out=minus_peak[:, j : j + 1], in_=s_bank[:], axis=mybir.AxisListType.X, op=ALU.min
            )
            nc.scalar.activation(
                out=exps[:, j, :],
                in_=s_bank[:],
                func=ACT.Exp,
                bias=minus_peak[:, j : j + 1],
                scale=-1.0,
                accum_out=total[:, j : j + 1],
            )
        transpose_w(0, range(4))
        empty_w_banks(0, range(4))

        attn_grouped = keep.tile([P, N_Q, PACK], BF16, align_bytes=64)

        def normalise(block):
            queries = slice(block * P, (block + 1) * P)
            nc.vector.tensor_tensor(
                out=attn_grouped[:, queries, :],
                in0=exps[:, :, queries].rearrange("p j n -> p n j"),
                in1=one_over_total[:].unsqueeze(1).to_broadcast([P, P, PACK]),
                op=ALU.mult,
            )

        def quantise_attn(block):
            queries = slice(block * P, (block + 1) * P)
            nc.vector.quantize_mx(
                out=attn_codes[:, queries].bitcast(FP8X4),
                scales=attn_scales[:, queries],
                in_=attn_grouped[:, queries, :].rearrange("p n j -> p (n j)"),
            )

        quantise_g(0)
        nc.vector.reciprocal(one_over_total[:], total[:])
        normalise(0)
        normalise(1)
        quantise_attn(0)
        normalise(2)
        quantise_attn(1)
        normalise(3)
        quantise_attn(2)
        quantise_attn(3)
        quantise_g(1)
        regroup_g(2)
        quantise_w(0, 0)

        y_early = []

        def project_some(chunk, tiles):
            if chunk >= 0:
                for i in tiles:
                    project_early(y_early[i], i, chunk)

        for c in range(N_CHUNKS):
            job = c // 2 + 1
            if c % 2 == 0:
                if c > 0:
                    regroup_g(c + 2)
                quantise_a(c - 1)
                quantise_g(c + 2)
                regroup_g(c + 3)
            for b in range(PACK):
                project_some(c - 2, (b,))
                make_a(c, b)
            if c == 0:
                bias_bank = y_banks.tile([P, P], BF16, name="y3")
                nc.tensor.transpose(bias_bank[:], bias_rows[:], ident_bf16[:])
                nc.vector.tensor_copy(out=bias_col[:], in_=bias_bank[:, 0:N_TILES])
            if c == 1:
                for i in range(EARLY_TILES):
                    y_early.append(y_banks.tile([P, N_Q], F32, name="y%d" % i))
            if c % 2 == 0:
                quantise_a(c)
                if c == 0:
                    quantise_w(0, 1)
                load_g(c // 2 + 3)
                if c // 2 + 3 <= N_UNITS:
                    load_w(c // 2 + 3)
                transpose_w(job, range(4))
                if c // 2 + 3 >= N_UNITS:
                    load_w(c // 2 + 4)
                empty_w_banks(job, range(4))
                quantise_g(c + 3)
                quantise_w(job, 0)
                quantise_w(job, 1)
            if c == GATE_CHUNK:
                gamma_sb = keep.tile([P, 1], BF16)
                nc.sync.dma_start(out=gamma_sb[:], in_=gamma.partition_broadcast(P))
            if c == GATE_CHUNK + 4:
                nc.sync.dma_start(out=x_sb[:], in_=x_rows)
                exp_minus_gamma = keep.tile([P, 1], F32)
                nc.scalar.activation(out=exp_minus_gamma[:], in_=gamma_sb[:], func=ACT.Exp, scale=-1.0)
                nc.vector.tensor_scalar_add(exp_minus_gamma[:], exp_minus_gamma[:], 1.0)
                nc.vector.reciprocal(alpha[:], exp_minus_gamma[:])
                nc.vector.tensor_scalar(
                    out=one_minus_alpha[:], in0=alpha[:], scalar1=-1.0, scalar2=1.0, op0=ALU.mult, op1=ALU.add
                )

        first, last = EARLY_TILES, EARLY_TILES + 1
        middle = N_CHUNKS // 2
        halves = (slice(0, N_Q // 2), slice(N_Q // 2, N_Q))
        quantise_a(N_CHUNKS - 1)
        project_some(N_CHUNKS - 2, range(EARLY_TILES))
        transpose_w(EARLY_JOBS + 1, range(4))
        empty_w_banks(EARLY_JOBS + 1, range(4))
        project_some(N_CHUNKS - 1, range(EARLY_TILES))
        quantise_w(EARLY_JOBS + 1, 0)
        quantise_w(EARLY_JOBS + 1, 1)
        for i in range(3):
            store_attn_g(y_early[i], i)
        transpose_w(EARLY_JOBS + 2, range(4))
        empty_w_banks(EARLY_JOBS + 2, range(4))
        weigh_x(0)
        store_out(0)
        quantise_w(EARLY_JOBS + 2, 0)
        weigh_x(1)
        store_out(1)
        quantise_w(EARLY_JOBS + 2, 1)
        y_first = y_banks.tile([P, N_Q], F32, name="y0")
        y_last = []
        for h in range(2):
            y_last.append(y_banks.tile([P, N_Q // 2], F32, name="y%d" % (1 + h)))
        for chunk in range(middle):
            project_late(y_first, first, chunk)
        transpose_w(EARLY_JOBS + 3, range(4))
        empty_w_banks(EARLY_JOBS + 3, range(4))
        quantise_w(EARLY_JOBS + 3, 0)
        weigh_x(2)
        store_out(2)
        quantise_w(EARLY_JOBS + 3, 1)
        store_attn_g(y_early[3], 3)
        weigh_x(3)
        store_out(3)
        for chunk in range(middle, N_CHUNKS):
            project_late(y_first, first, chunk)
        store_attn_g(y_first, first)
        weigh_x(first)
        store_out(first)
        for h in range(2):
            weigh_x(last, halves[h])
        for h in range(2):
            for chunk in range(N_CHUNKS):
                project_late(y_last[h], last, chunk, halves[h])
            store_attn_g(y_last[h], last, halves[h])
            store_out(last, halves[h])
